import numpy as np
import ml_dtypes

BF16 = ml_dtypes.bfloat16


def bf(x):
    return np.asarray(x, np.float32).astype(BF16)


def f32(x):
    return np.asarray(x, np.float32)


def f64(x):
    return np.asarray(x).astype(np.float64)


def striped(idx):
    return np.tile(idx.reshape(-1, 16).T, (8, 1))


C, S, B, L, W, N = 128, 1024, 16, 32, 4, 2048


def setup_inputs():
    return {
        "table": f32(0.5 * np.random.standard_normal((C, S))),
        "ta": f32(0.5 * np.random.standard_normal((C, L))),
        "tc": f32(0.5 * np.random.standard_normal((C, L))),
        "u": f32(0.1 * np.random.standard_normal((C, B))),
        "offs": striped(np.random.permutation(np.tile(np.arange(S), 2))[:N]),
    }


def reference(table, ta, tc, u, offs):
    idx = offs[:16].T.reshape(-1)
    bag = f64(table)[:, idx].reshape(C, W, B, L).sum(axis=1)
    m = bag + f64(ta)[:, None, :]
    c = bag + f64(tc)[:, None, :]
    score = (m * f64(u)[:, :, None]).sum(axis=0)
    ex = np.exp(score)
    p = ex / ex.sum(axis=1, keepdims=True)
    return (c * p[None, :, :]).sum(axis=2) + f64(u)

@@ -1,0 +1,86 @@
+import concourse.mybir as mybir
+
+F32 = mybir.dt.float32
+BF16 = mybir.dt.bfloat16
+U16 = mybir.dt.uint16
+ADD = mybir.AluOpType.add
+MULT = mybir.AluOpType.mult
+MAX = mybir.AluOpType.max
+EXP = mybir.ActivationFunctionType.Exp
+X = mybir.AxisListType.X
+
+FEATURES = 128
+VOCAB = 1024
+STORIES = 16
+SLOTS = 32
+WORDS = 4
+SENTENCES = STORIES * SLOTS
+OFFSET_COLUMNS = SENTENCES // 16
+LOAD_PIECES = 4
+
+FLOPS = 2 * FEATURES * SENTENCES * 2
+
+
+def tile_memnnlayer_kernel(tc, table, ta, tc_enc, u, offs, out):
+    nc = tc.nc
+    with tc.tile_pool(name="held", bufs=1) as held, tc.psum_pool(name="psum", bufs=1) as psum:
+        offsets = held.tile([FEATURES, WORDS * OFFSET_COLUMNS], U16, name="offsets")
+        nc.sync.dma_start(offsets[:], offs)
+        words = held.tile([FEATURES, VOCAB], F32, name="words")
+        width = VOCAB // LOAD_PIECES
+        for i in range(LOAD_PIECES):
+            queue = nc.scalar if i % 2 == 0 else nc.sync
+            queue.dma_start(words[:, i * width : (i + 1) * width], table[:, i * width : (i + 1) * width])
+        key_time = held.tile([FEATURES, SLOTS], F32, name="key_time")
+        nc.gpsimd.dma_start(key_time[:], ta)
+        value_time = held.tile([FEATURES, SLOTS], F32, name="value_time")
+        nc.gpsimd.dma_start(value_time[:], tc_enc)
+        state = held.tile([FEATURES, STORIES], F32, name="state")
+        nc.gpsimd.dma_start(state[:], u)
+
+        def by_story(ap):
+            return ap.rearrange("e (b s) -> e b s", s=SLOTS)
+
+        def over_stories(ap):
+            return ap.unsqueeze(1).to_broadcast([FEATURES, STORIES, SLOTS])
+
+        def over_slots(ap):
+            return ap.unsqueeze(2).to_broadcast([FEATURES, STORIES, SLOTS])
+
+        key_time_all = held.tile([FEATURES, SENTENCES], F32, name="key_time_all")
+        nc.vector.tensor_copy(by_story(key_time_all[:]), over_stories(key_time[:]))
+        time_shift = held.tile([FEATURES, SLOTS], F32, name="time_shift")
+        nc.vector.tensor_sub(time_shift[:], value_time[:], key_time[:])
+        ones = held.tile([FEATURES, FEATURES], BF16, name="ones")
+        nc.vector.memset(ones[:], 1.0)
+
+        sums = [held.tile([FEATURES, SENTENCES], F32, name=f"sums{i}") for i in range(2)]
+        keys = key_time_all
+        for t in range(WORDS):
+            picked = words[:].indirect(offsets[:, t * OFFSET_COLUMNS : (t + 1) * OFFSET_COLUMNS])
+            nc.vector.tensor_tensor(sums[t % 2][:], picked, keys[:], ADD)
+            keys = sums[t % 2]
+
+        values = held.tile([FEATURES, SENTENCES], F32, name="values")
+        nc.gpsimd.tensor_tensor(by_story(values[:]), by_story(keys[:]), over_stories(time_shift[:]), ADD)
+
+        products = held.tile([FEATURES, SENTENCES], BF16, name="products")
+        nc.vector.tensor_tensor(by_story(products[:]), by_story(keys[:]), over_slots(state[:]), MULT)
+        score = psum.tile([FEATURES, SENTENCES], F32, name="score")
+        nc.tensor.matmul(score[:], ones[:], products[:], start=True, stop=True)
+
+        neg_max = held.tile([FEATURES, STORIES], F32, name="neg_max")
+        nc.vector.tensor_reduce(neg_max[:], by_story(score[:]), axis=X, op=MAX, negate=True)
+        weights = held.tile([FEATURES, SENTENCES], F32, name="weights")
+        nc.vector.tensor_tensor(by_story(weights[:]), by_story(score[:]), over_slots(neg_max[:]), ADD)
+        nc.scalar.activation(weights[:], weights[:], EXP)
+        total = held.tile([FEATURES, STORIES], F32, name="total")
+        nc.vector.tensor_reduce(total[:], by_story(weights[:]), axis=X, op=ADD)
+
+        nc.vector.tensor_tensor(values[:], values[:], weights[:], MULT)
+        answer = held.tile([FEATURES, STORIES], F32, name="answer")
+        nc.vector.tensor_reduce(answer[:], by_story(values[:]), axis=X, op=ADD)
+        nc.vector.reciprocal(total[:], total[:])
+        nc.vector.tensor_tensor(answer[:], answer[:], total[:], MULT)
+        nc.vector.tensor_tensor(answer[:], answer[:], state[:], ADD)
+        nc.sync.dma_start(out, answer[:])

@@ -1,86 +1,128 @@
 import concourse.mybir as mybir
+from concourse.masks import make_identity
 
 F32 = mybir.dt.float32
 BF16 = mybir.dt.bfloat16
 U16 = mybir.dt.uint16
 ADD = mybir.AluOpType.add
+SUBTRACT = mybir.AluOpType.subtract
 MULT = mybir.AluOpType.mult
 MAX = mybir.AluOpType.max
+NOT_EQUAL = mybir.AluOpType.not_equal
 EXP = mybir.ActivationFunctionType.Exp
 X = mybir.AxisListType.X
 
-FEATURES = 128
+P = 128
 VOCAB = 1024
 STORIES = 16
 SLOTS = 32
 WORDS = 4
 SENTENCES = STORIES * SLOTS
-OFFSET_COLUMNS = SENTENCES // 16
+GROUP = P // SLOTS
+GROUPS = STORIES // GROUP
 LOAD_PIECES = 4
 
-FLOPS = 2 * FEATURES * SENTENCES * 2
+FLOPS = 2 * P * SENTENCES * 2
 
 
 def tile_memnnlayer_kernel(tc, table, ta, tc_enc, u, offs, out):
     nc = tc.nc
     with tc.tile_pool(name="held", bufs=1) as held, tc.psum_pool(name="psum", bufs=1) as psum:
-        offsets = held.tile([FEATURES, WORDS * OFFSET_COLUMNS], U16, name="offsets")
+        offsets = held.tile([P, WORDS * SENTENCES // 16], U16, name="offsets")
         nc.sync.dma_start(offsets[:], offs)
-        words = held.tile([FEATURES, VOCAB], F32, name="words")
+        state = held.tile([P, STORIES], F32, name="state")
+        nc.scalar.dma_start(state[:], u)
+        value_time = held.tile([P, SLOTS], F32, name="value_time")
+        nc.sync.dma_start(value_time[:], tc_enc)
+        key_time = held.tile([P, SLOTS], F32, name="key_time")
+        nc.scalar.dma_start(key_time[:], ta)
+        words = held.tile([P, VOCAB], F32, name="words")
         width = VOCAB // LOAD_PIECES
         for i in range(LOAD_PIECES):
-            queue = nc.scalar if i % 2 == 0 else nc.sync
+            queue = nc.sync if i % 2 == 0 else nc.scalar
             queue.dma_start(words[:, i * width : (i + 1) * width], table[:, i * width : (i + 1) * width])
-        key_time = held.tile([FEATURES, SLOTS], F32, name="key_time")
-        nc.gpsimd.dma_start(key_time[:], ta)
-        value_time = held.tile([FEATURES, SLOTS], F32, name="value_time")
-        nc.gpsimd.dma_start(value_time[:], tc_enc)
-        state = held.tile([FEATURES, STORIES], F32, name="state")
-        nc.gpsimd.dma_start(state[:], u)
 
-        def by_story(ap):
-            return ap.rearrange("e (b s) -> e b s", s=SLOTS)
+        warm = held.tile([P, 1], F32, name="warm")
+        nc.vector.memset(warm[:], 0.0)
+        nc.scalar.activation(warm[:], warm[:], EXP)
+        identity = held.tile([P, P], F32, name="identity")
+        make_identity(nc, identity[:])
+        row_is_story = held.tile([P, STORIES], F32, name="row_is_story")
+        nc.gpsimd.memset(row_is_story[:], 0.0)
+        nc.gpsimd.affine_select(
+            out=row_is_story[:],
+            in_=row_is_story[:],
+            pattern=[[-GROUP, GROUPS], [-(SLOTS + 1), GROUP]],
+            compare_op=NOT_EQUAL,
+            fill=1.0,
+            base=0,
+            channel_multiplier=1,
+        )
+        row_in_use = held.tile([P, 1], F32, name="row_in_use")
+        nc.vector.tensor_reduce(row_in_use[:], row_is_story[:], axis=X, op=ADD)
+        spread_state = held.tile([P, STORIES * P], BF16, name="spread_state")
+        nc.vector.memset(spread_state[:], 0.0)
+        for b in range(STORIES):
+            column = b * P + SLOTS * (b % GROUP) + b
+            nc.scalar.copy(spread_state[:, column : column + 1], state[:, b : b + 1])
+        value_time_all = held.tile([P, SENTENCES], F32, name="value_time_all")
+        nc.vector.tensor_copy(
+            value_time_all[:].rearrange("e (b s) -> e b s", s=SLOTS),
+            value_time[:].unsqueeze(1).to_broadcast([P, STORIES, SLOTS]),
+        )
+        key_shift = held.tile([P, GROUP * SLOTS], F32, name="key_shift")
+        nc.vector.tensor_tensor(
+            key_shift[:].rearrange("e (j s) -> e j s", s=SLOTS),
+            key_time[:].unsqueeze(1).to_broadcast([P, GROUP, SLOTS]),
+            value_time[:].unsqueeze(1).to_broadcast([P, GROUP, SLOTS]),
+            SUBTRACT,
+        )
 
-        def over_stories(ap):
-            return ap.unsqueeze(1).to_broadcast([FEATURES, STORIES, SLOTS])
-
-        def over_slots(ap):
-            return ap.unsqueeze(2).to_broadcast([FEATURES, STORIES, SLOTS])
-
-        key_time_all = held.tile([FEATURES, SENTENCES], F32, name="key_time_all")
-        nc.vector.tensor_copy(by_story(key_time_all[:]), over_stories(key_time[:]))
-        time_shift = held.tile([FEATURES, SLOTS], F32, name="time_shift")
-        nc.vector.tensor_sub(time_shift[:], value_time[:], key_time[:])
-        ones = held.tile([FEATURES, FEATURES], BF16, name="ones")
-        nc.vector.memset(ones[:], 1.0)
-
-        sums = [held.tile([FEATURES, SENTENCES], F32, name=f"sums{i}") for i in range(2)]
-        keys = key_time_all
+        sums = [held.tile([P, SENTENCES], F32, name=f"sums{i}") for i in range(2)]
+        values = value_time_all
         for t in range(WORDS):
-            picked = words[:].indirect(offsets[:, t * OFFSET_COLUMNS : (t + 1) * OFFSET_COLUMNS])
-            nc.vector.tensor_tensor(sums[t % 2][:], picked, keys[:], ADD)
-            keys = sums[t % 2]
+            for g in range(GROUPS):
+                columns = slice(g * P, (g + 1) * P)
+                first = (t * SENTENCES + g * P) // 16
+                picked = words[:].indirect(offsets[:, first : first + P // 16])
+                nc.vector.tensor_tensor(sums[t % 2][:, columns], picked, values[:, columns], ADD)
+            values = sums[t % 2]
 
-        values = held.tile([FEATURES, SENTENCES], F32, name="values")
-        nc.gpsimd.tensor_tensor(by_story(values[:]), by_story(keys[:]), over_stories(time_shift[:]), ADD)
+        keys = held.tile([P, SENTENCES], BF16, name="keys")
+        score = psum.tile([P, SLOTS], F32, name="score")
+        values_t = held.tile([P, SENTENCES], F32, name="values_t")
+        for g in range(GROUPS):
+            columns = slice(g * P, (g + 1) * P)
+            adder = nc.vector if g == GROUPS - 1 else nc.gpsimd
+            adder.tensor_tensor(keys[:, columns], values[:, columns], key_shift[:], ADD)
+            for b in range(g * GROUP, (g + 1) * GROUP):
+                nc.tensor.matmul(
+                    score[:],
+                    spread_state[:, b * P : (b + 1) * P],
+                    keys[:, b * SLOTS : (b + 1) * SLOTS],
+                    start=(b == 0),
+                    stop=(b == STORIES - 1),
+                )
+            turned = psum.tile([P, P], F32, name=f"turned{g}")
+            nc.tensor.transpose(turned[:], values[:, columns], identity[:])
+            nc.scalar.copy(values_t[:, columns], turned[:])
 
-        products = held.tile([FEATURES, SENTENCES], BF16, name="products")
-        nc.vector.tensor_tensor(by_story(products[:]), by_story(keys[:]), over_slots(state[:]), MULT)
-        score = psum.tile([FEATURES, SENTENCES], F32, name="score")
-        nc.tensor.matmul(score[:], ones[:], products[:], start=True, stop=True)
+        neg_max = held.tile([P, 1], F32, name="neg_max")
+        nc.vector.tensor_reduce(neg_max[:], score[:], axis=X, op=MAX, negate=True)
+        weights = held.tile([P, SLOTS], F32, name="weights")
+        total = held.tile([P, 1], F32, name="total")
+        nc.scalar.activation(weights[:], score[:], EXP, bias=neg_max[:], accum_out=total[:])
+        inverse = held.tile([P, 1], F32, name="inverse")
+        nc.vector.reciprocal(inverse[:], total[:])
+        shares = held.tile([P, SLOTS], F32, name="shares", align_bytes=64)
+        nc.vector.tensor_scalar(shares[:], weights[:], inverse[:], row_in_use[:], MULT, MULT)
+        shares_t = held.tile([P, SLOTS], F32, name="shares_t", align_bytes=64)
+        nc.vector.transpose(shares_t[:], shares[:])
 
-        neg_max = held.tile([FEATURES, STORIES], F32, name="neg_max")
-        nc.vector.tensor_reduce(neg_max[:], by_story(score[:]), axis=X, op=MAX, negate=True)
-        weights = held.tile([FEATURES, SENTENCES], F32, name="weights")
-        nc.vector.tensor_tensor(by_story(weights[:]), by_story(score[:]), over_slots(neg_max[:]), ADD)
-        nc.scalar.activation(weights[:], weights[:], EXP)
-        total = held.tile([FEATURES, STORIES], F32, name="total")
-        nc.vector.tensor_reduce(total[:], by_story(weights[:]), axis=X, op=ADD)
-
-        nc.vector.tensor_tensor(values[:], values[:], weights[:], MULT)
-        answer = held.tile([FEATURES, STORIES], F32, name="answer")
-        nc.vector.tensor_reduce(answer[:], by_story(values[:]), axis=X, op=ADD)
-        nc.vector.reciprocal(total[:], total[:])
-        nc.vector.tensor_tensor(answer[:], answer[:], total[:], MULT)
-        nc.vector.tensor_tensor(answer[:], answer[:], state[:], ADD)
+        mixed = psum.tile([P, STORIES], F32, name="mixed")
+        for g in range(GROUPS):
+            stories = slice(g * GROUP, (g + 1) * GROUP)
+            nc.tensor.matmul(mixed[:, stories], values_t[:, g * P : (g + 1) * P], shares_t[:, stories], start=True, stop=True)
+        answer = held.tile([P, STORIES], F32, name="answer")
+        nc.vector.tensor_tensor(answer[:], mixed[:], state[:], ADD)
         nc.sync.dma_start(out, answer[:])

@@ -30,10 +30,6 @@ def tile_memnnlayer_kernel(tc, table, ta, tc_enc, u, offs, out):
     with tc.tile_pool(name="held", bufs=1) as held, tc.psum_pool(name="psum", bufs=1) as psum:
         offsets = held.tile([P, WORDS * SENTENCES // 16], U16, name="offsets")
         nc.sync.dma_start(offsets[:], offs)
-        state = held.tile([P, STORIES], F32, name="state")
-        nc.scalar.dma_start(state[:], u)
-        value_time = held.tile([P, SLOTS], F32, name="value_time")
-        nc.sync.dma_start(value_time[:], tc_enc)
         key_time = held.tile([P, SLOTS], F32, name="key_time")
         nc.scalar.dma_start(key_time[:], ta)
         words = held.tile([P, VOCAB], F32, name="words")
@@ -41,10 +37,24 @@ def tile_memnnlayer_kernel(tc, table, ta, tc_enc, u, offs, out):
         for i in range(LOAD_PIECES):
             queue = nc.sync if i % 2 == 0 else nc.scalar
             queue.dma_start(words[:, i * width : (i + 1) * width], table[:, i * width : (i + 1) * width])
+        state = held.tile([P, STORIES], F32, name="state")
+        nc.sync.dma_start(state[:], u)
+        value_time = held.tile([P, SLOTS], F32, name="value_time")
+        nc.scalar.dma_start(value_time[:], tc_enc)
 
         warm = held.tile([P, 1], F32, name="warm")
         nc.vector.memset(warm[:], 0.0)
         nc.scalar.activation(warm[:], warm[:], EXP)
+        key_time_all = held.tile([P, SENTENCES], F32, name="key_time_all")
+        nc.vector.tensor_copy(
+            key_time_all[:].rearrange("e (b s) -> e b s", s=SLOTS),
+            key_time[:].unsqueeze(1).to_broadcast([P, STORIES, SLOTS]),
+        )
+        spread_state = held.tile([P, STORIES * P], BF16, name="spread_state")
+        nc.gpsimd.memset(spread_state[:], 0.0)
+        for b in range(STORIES):
+            column = b * P + SLOTS * (b % GROUP) + b
+            nc.scalar.copy(spread_state[:, column : column + 1], state[:, b : b + 1])
         identity = held.tile([P, P], F32, name="identity")
         make_identity(nc, identity[:])
         row_is_story = held.tile([P, STORIES], F32, name="row_is_story")
@@ -60,49 +70,41 @@ def tile_memnnlayer_kernel(tc, table, ta, tc_enc, u, offs, out):
         )
         row_in_use = held.tile([P, 1], F32, name="row_in_use")
         nc.vector.tensor_reduce(row_in_use[:], row_is_story[:], axis=X, op=ADD)
-        spread_state = held.tile([P, STORIES * P], BF16, name="spread_state")
-        nc.vector.memset(spread_state[:], 0.0)
-        for b in range(STORIES):
-            column = b * P + SLOTS * (b % GROUP) + b
-            nc.scalar.copy(spread_state[:, column : column + 1], state[:, b : b + 1])
-        value_time_all = held.tile([P, SENTENCES], F32, name="value_time_all")
-        nc.vector.tensor_copy(
-            value_time_all[:].rearrange("e (b s) -> e b s", s=SLOTS),
-            value_time[:].unsqueeze(1).to_broadcast([P, STORIES, SLOTS]),
-        )
-        key_shift = held.tile([P, GROUP * SLOTS], F32, name="key_shift")
-        nc.vector.tensor_tensor(
-            key_shift[:].rearrange("e (j s) -> e j s", s=SLOTS),
-            key_time[:].unsqueeze(1).to_broadcast([P, GROUP, SLOTS]),
+        value_shift = held.tile([P, GROUP * SLOTS], F32, name="value_shift")
+        nc.gpsimd.tensor_tensor(
+            value_shift[:].rearrange("e (j s) -> e j s", s=SLOTS),
             value_time[:].unsqueeze(1).to_broadcast([P, GROUP, SLOTS]),
+            key_time[:].unsqueeze(1).to_broadcast([P, GROUP, SLOTS]),
             SUBTRACT,
         )
 
         sums = [held.tile([P, SENTENCES], F32, name=f"sums{i}") for i in range(2)]
-        values = value_time_all
+        keys = key_time_all
         for t in range(WORDS):
-            for g in range(GROUPS):
-                columns = slice(g * P, (g + 1) * P)
-                first = (t * SENTENCES + g * P) // 16
-                picked = words[:].indirect(offsets[:, first : first + P // 16])
-                nc.vector.tensor_tensor(sums[t % 2][:, columns], picked, values[:, columns], ADD)
-            values = sums[t % 2]
+            width = P if t == WORDS - 1 else SENTENCES
+            for start in range(0, SENTENCES, width):
+                columns = slice(start, start + width)
+                first = (t * SENTENCES + start) // 16
+                picked = words[:].indirect(offsets[:, first : first + width // 16])
+                nc.vector.tensor_tensor(sums[t % 2][:, columns], picked, keys[:, columns], ADD)
+            keys = sums[t % 2]
 
-        keys = held.tile([P, SENTENCES], BF16, name="keys")
+        keys_bf = held.tile([P, SENTENCES], BF16, name="keys_bf")
         score = psum.tile([P, SLOTS], F32, name="score")
+        values = held.tile([P, SENTENCES], F32, name="values")
         values_t = held.tile([P, SENTENCES], F32, name="values_t")
         for g in range(GROUPS):
             columns = slice(g * P, (g + 1) * P)
-            adder = nc.vector if g == GROUPS - 1 else nc.gpsimd
-            adder.tensor_tensor(keys[:, columns], values[:, columns], key_shift[:], ADD)
+            nc.scalar.copy(keys_bf[:, columns], keys[:, columns])
             for b in range(g * GROUP, (g + 1) * GROUP):
                 nc.tensor.matmul(
                     score[:],
                     spread_state[:, b * P : (b + 1) * P],
-                    keys[:, b * SLOTS : (b + 1) * SLOTS],
+                    keys_bf[:, b * SLOTS : (b + 1) * SLOTS],
                     start=(b == 0),
                     stop=(b == STORIES - 1),
                 )
+            nc.gpsimd.tensor_tensor(values[:, columns], keys[:, columns], value_shift[:], ADD)
             turned = psum.tile([P, P], F32, name=f"turned{g}")
             nc.tensor.transpose(turned[:], values[:, columns], identity[:])
             nc.scalar.copy(values_t[:, columns], turned[:])

@@ -10,6 +10,7 @@ MULT = mybir.AluOpType.mult
 MAX = mybir.AluOpType.max
 NOT_EQUAL = mybir.AluOpType.not_equal
 EXP = mybir.ActivationFunctionType.Exp
+COPY = mybir.ActivationFunctionType.Copy
 X = mybir.AxisListType.X
 
 P = 128
@@ -32,15 +33,15 @@ def tile_memnnlayer_kernel(tc, table, ta, tc_enc, u, offs, out):
         nc.sync.dma_start(offsets[:], offs)
         key_time = held.tile([P, SLOTS], F32, name="key_time")
         nc.scalar.dma_start(key_time[:], ta)
+        value_time = held.tile([P, SLOTS], F32, name="value_time")
+        nc.sync.dma_start(value_time[:], tc_enc)
+        state = held.tile([P, STORIES], F32, name="state")
+        nc.scalar.dma_start(state[:], u)
         words = held.tile([P, VOCAB], F32, name="words")
-        width = VOCAB // LOAD_PIECES
+        piece = VOCAB // LOAD_PIECES
         for i in range(LOAD_PIECES):
             queue = nc.sync if i % 2 == 0 else nc.scalar
-            queue.dma_start(words[:, i * width : (i + 1) * width], table[:, i * width : (i + 1) * width])
-        state = held.tile([P, STORIES], F32, name="state")
-        nc.sync.dma_start(state[:], u)
-        value_time = held.tile([P, SLOTS], F32, name="value_time")
-        nc.scalar.dma_start(value_time[:], tc_enc)
+            queue.dma_start(words[:, i * piece : (i + 1) * piece], table[:, i * piece : (i + 1) * piece])
 
         warm = held.tile([P, 1], F32, name="warm")
         nc.vector.memset(warm[:], 0.0)
@@ -51,7 +52,7 @@ def tile_memnnlayer_kernel(tc, table, ta, tc_enc, u, offs, out):
             key_time[:].unsqueeze(1).to_broadcast([P, STORIES, SLOTS]),
         )
         spread_state = held.tile([P, STORIES * P], BF16, name="spread_state")
-        nc.gpsimd.memset(spread_state[:], 0.0)
+        nc.vector.memset(spread_state[:].bitcast(F32), 0.0)
         for b in range(STORIES):
             column = b * P + SLOTS * (b % GROUP) + b
             nc.scalar.copy(spread_state[:, column : column + 1], state[:, b : b + 1])
@@ -69,14 +70,18 @@ def tile_memnnlayer_kernel(tc, table, ta, tc_enc, u, offs, out):
             channel_multiplier=1,
         )
         row_in_use = held.tile([P, 1], F32, name="row_in_use")
-        nc.vector.tensor_reduce(row_in_use[:], row_is_story[:], axis=X, op=ADD)
+        nc.scalar.activation(row_is_story[:], row_is_story[:], COPY, accum_out=row_in_use[:])
         value_shift = held.tile([P, GROUP * SLOTS], F32, name="value_shift")
-        nc.gpsimd.tensor_tensor(
+        nc.vector.tensor_tensor(
             value_shift[:].rearrange("e (j s) -> e j s", s=SLOTS),
             value_time[:].unsqueeze(1).to_broadcast([P, GROUP, SLOTS]),
             key_time[:].unsqueeze(1).to_broadcast([P, GROUP, SLOTS]),
             SUBTRACT,
         )
+
+        turned = [psum.tile([P, P], F32, name=f"turned{g}") for g in range(GROUPS)]
+        for g in range(GROUPS):
+            nc.tensor.matmul(turned[g][:], value_shift[:], identity[:], is_transpose=True, start=True, stop=False)
 
         sums = [held.tile([P, SENTENCES], F32, name=f"sums{i}") for i in range(2)]
         keys = key_time_all
@@ -91,7 +96,6 @@ def tile_memnnlayer_kernel(tc, table, ta, tc_enc, u, offs, out):
 
         keys_bf = held.tile([P, SENTENCES], BF16, name="keys_bf")
         score = psum.tile([P, SLOTS], F32, name="score")
-        values = held.tile([P, SENTENCES], F32, name="values")
         values_t = held.tile([P, SENTENCES], F32, name="values_t")
         for g in range(GROUPS):
             columns = slice(g * P, (g + 1) * P)
@@ -104,10 +108,8 @@ def tile_memnnlayer_kernel(tc, table, ta, tc_enc, u, offs, out):
                     start=(b == 0),
                     stop=(b == STORIES - 1),
                 )
-            nc.gpsimd.tensor_tensor(values[:, columns], keys[:, columns], value_shift[:], ADD)
-            turned = psum.tile([P, P], F32, name=f"turned{g}")
-            nc.tensor.transpose(turned[:], values[:, columns], identity[:])
-            nc.scalar.copy(values_t[:, columns], turned[:])
+            nc.tensor.matmul(turned[g][:], keys[:, columns], identity[:], is_transpose=True, start=False, stop=True)
+            nc.scalar.copy(values_t[:, columns], turned[g][:])
 
         neg_max = held.tile([P, 1], F32, name="neg_max")
         nc.vector.tensor_reduce(neg_max[:], score[:], axis=X, op=MAX, negate=True)

@@ -1,5 +1,4 @@
 import concourse.mybir as mybir
-from concourse.masks import make_identity
 
 F32 = mybir.dt.float32
 BF16 = mybir.dt.bfloat16
@@ -8,7 +7,6 @@ ADD = mybir.AluOpType.add
 SUBTRACT = mybir.AluOpType.subtract
 MULT = mybir.AluOpType.mult
 MAX = mybir.AluOpType.max
-NOT_EQUAL = mybir.AluOpType.not_equal
 EXP = mybir.ActivationFunctionType.Exp
 COPY = mybir.ActivationFunctionType.Copy
 X = mybir.AxisListType.X
@@ -19,8 +17,9 @@ STORIES = 16
 SLOTS = 32
 WORDS = 4
 SENTENCES = STORIES * SLOTS
-GROUP = P // SLOTS
+GROUP = 4
 GROUPS = STORIES // GROUP
+GROUP_COLUMNS = GROUP * SLOTS
 LOAD_PIECES = 4
 
 FLOPS = 2 * P * SENTENCES * 2
@@ -33,60 +32,40 @@ def tile_memnnlayer_kernel(tc, table, ta, tc_enc, u, offs, out):
         nc.sync.dma_start(offsets[:], offs)
         key_time = held.tile([P, SLOTS], F32, name="key_time")
         nc.scalar.dma_start(key_time[:], ta)
-        value_time = held.tile([P, SLOTS], F32, name="value_time")
-        nc.sync.dma_start(value_time[:], tc_enc)
-        state = held.tile([P, STORIES], F32, name="state")
-        nc.scalar.dma_start(state[:], u)
         words = held.tile([P, VOCAB], F32, name="words")
         piece = VOCAB // LOAD_PIECES
         for i in range(LOAD_PIECES):
             queue = nc.sync if i % 2 == 0 else nc.scalar
             queue.dma_start(words[:, i * piece : (i + 1) * piece], table[:, i * piece : (i + 1) * piece])
+        state = held.tile([P, STORIES], F32, name="state")
+        nc.sync.dma_start(state[:], u)
+        value_time = held.tile([P, SLOTS], F32, name="value_time")
+        nc.scalar.dma_start(value_time[:], tc_enc)
+
+        def by_story(ap):
+            return ap.rearrange("e (b s) -> e b s", s=SLOTS)
 
         warm = held.tile([P, 1], F32, name="warm")
         nc.vector.memset(warm[:], 0.0)
         nc.scalar.activation(warm[:], warm[:], EXP)
         key_time_all = held.tile([P, SENTENCES], F32, name="key_time_all")
-        nc.vector.tensor_copy(
-            key_time_all[:].rearrange("e (b s) -> e b s", s=SLOTS),
-            key_time[:].unsqueeze(1).to_broadcast([P, STORIES, SLOTS]),
-        )
-        spread_state = held.tile([P, STORIES * P], BF16, name="spread_state")
-        nc.vector.memset(spread_state[:].bitcast(F32), 0.0)
-        for b in range(STORIES):
-            column = b * P + SLOTS * (b % GROUP) + b
-            nc.scalar.copy(spread_state[:, column : column + 1], state[:, b : b + 1])
-        identity = held.tile([P, P], F32, name="identity")
-        make_identity(nc, identity[:])
-        row_is_story = held.tile([P, STORIES], F32, name="row_is_story")
-        nc.gpsimd.memset(row_is_story[:], 0.0)
-        nc.gpsimd.affine_select(
-            out=row_is_story[:],
-            in_=row_is_story[:],
-            pattern=[[-GROUP, GROUPS], [-(SLOTS + 1), GROUP]],
-            compare_op=NOT_EQUAL,
-            fill=1.0,
-            base=0,
-            channel_multiplier=1,
-        )
-        row_in_use = held.tile([P, 1], F32, name="row_in_use")
-        nc.scalar.activation(row_is_story[:], row_is_story[:], COPY, accum_out=row_in_use[:])
-        value_shift = held.tile([P, GROUP * SLOTS], F32, name="value_shift")
-        nc.vector.tensor_tensor(
-            value_shift[:].rearrange("e (j s) -> e j s", s=SLOTS),
+        nc.vector.tensor_copy(by_story(key_time_all[:]), key_time[:].unsqueeze(1).to_broadcast([P, STORIES, SLOTS]))
+        value_shift = held.tile([P, GROUP_COLUMNS], F32, name="value_shift")
+        nc.gpsimd.tensor_tensor(
+            by_story(value_shift[:]),
             value_time[:].unsqueeze(1).to_broadcast([P, GROUP, SLOTS]),
             key_time[:].unsqueeze(1).to_broadcast([P, GROUP, SLOTS]),
             SUBTRACT,
         )
-
-        turned = [psum.tile([P, P], F32, name=f"turned{g}") for g in range(GROUPS)]
-        for g in range(GROUPS):
-            nc.tensor.matmul(turned[g][:], value_shift[:], identity[:], is_transpose=True, start=True, stop=False)
+        state_wide = held.tile([P, STORIES * P], BF16, name="state_wide")
+        nc.scalar.activation(
+            state_wide[:].rearrange("e (b r) -> e b r", r=P), state[:].unsqueeze(2).to_broadcast([P, STORIES, P]), COPY
+        )
 
         sums = [held.tile([P, SENTENCES], F32, name=f"sums{i}") for i in range(2)]
         keys = key_time_all
         for t in range(WORDS):
-            width = P if t == WORDS - 1 else SENTENCES
+            width = GROUP_COLUMNS if t == WORDS - 1 else SENTENCES
             for start in range(0, SENTENCES, width):
                 columns = slice(start, start + width)
                 first = (t * SENTENCES + start) // 16
@@ -95,38 +74,42 @@ def tile_memnnlayer_kernel(tc, table, ta, tc_enc, u, offs, out):
             keys = sums[t % 2]
 
         keys_bf = held.tile([P, SENTENCES], BF16, name="keys_bf")
-        score = psum.tile([P, SLOTS], F32, name="score")
-        values_t = held.tile([P, SENTENCES], F32, name="values_t")
+        values = held.tile([P, SENTENCES], F32, name="values")
+        weights = held.tile([P, SENTENCES], F32, name="weights")
+        neg_max = held.tile([P, STORIES], F32, name="neg_max")
+        total = held.tile([P, STORIES], F32, name="total")
+        mixed = held.tile([P, STORIES], F32, name="mixed")
         for g in range(GROUPS):
-            columns = slice(g * P, (g + 1) * P)
-            nc.scalar.copy(keys_bf[:, columns], keys[:, columns])
-            for b in range(g * GROUP, (g + 1) * GROUP):
-                nc.tensor.matmul(
-                    score[:],
-                    spread_state[:, b * P : (b + 1) * P],
-                    keys_bf[:, b * SLOTS : (b + 1) * SLOTS],
-                    start=(b == 0),
-                    stop=(b == STORIES - 1),
-                )
-            nc.tensor.matmul(turned[g][:], keys[:, columns], identity[:], is_transpose=True, start=False, stop=True)
-            nc.scalar.copy(values_t[:, columns], turned[g][:])
-
-        neg_max = held.tile([P, 1], F32, name="neg_max")
-        nc.vector.tensor_reduce(neg_max[:], score[:], axis=X, op=MAX, negate=True)
-        weights = held.tile([P, SLOTS], F32, name="weights")
-        total = held.tile([P, 1], F32, name="total")
-        nc.scalar.activation(weights[:], score[:], EXP, bias=neg_max[:], accum_out=total[:])
-        inverse = held.tile([P, 1], F32, name="inverse")
-        nc.vector.reciprocal(inverse[:], total[:])
-        shares = held.tile([P, SLOTS], F32, name="shares", align_bytes=64)
-        nc.vector.tensor_scalar(shares[:], weights[:], inverse[:], row_in_use[:], MULT, MULT)
-        shares_t = held.tile([P, SLOTS], F32, name="shares_t", align_bytes=64)
-        nc.vector.transpose(shares_t[:], shares[:])
-
-        mixed = psum.tile([P, STORIES], F32, name="mixed")
-        for g in range(GROUPS):
+            columns = slice(g * GROUP_COLUMNS, (g + 1) * GROUP_COLUMNS)
             stories = slice(g * GROUP, (g + 1) * GROUP)
-            nc.tensor.matmul(mixed[:, stories], values_t[:, g * P : (g + 1) * P], shares_t[:, stories], start=True, stop=True)
+            nc.scalar.copy(keys_bf[:, columns], keys[:, columns])
+            nc.gpsimd.tensor_tensor(values[:, columns], keys[:, columns], value_shift[:], ADD)
+            score = psum.tile([P, GROUP_COLUMNS], F32, name=f"score{g}")
+            for j in range(GROUP):
+                b = g * GROUP + j
+                nc.tensor.matmul(
+                    score[:, j * SLOTS : (j + 1) * SLOTS],
+                    state_wide[:, b * P : (b + 1) * P],
+                    keys_bf[:, b * SLOTS : (b + 1) * SLOTS],
+                    start=True,
+                    stop=True,
+                )
+            nc.vector.tensor_reduce(neg_max[:, stories], by_story(score[:]), axis=X, op=MAX, negate=True)
+            for j in range(GROUP):
+                b = g * GROUP + j
+                nc.scalar.activation(
+                    weights[:, b * SLOTS : (b + 1) * SLOTS],
+                    score[:, j * SLOTS : (j + 1) * SLOTS],
+                    EXP,
+                    bias=neg_max[:, b : b + 1],
+                    accum_out=total[:, b : b + 1],
+                )
+            nc.vector.tensor_tensor(values[:, columns], values[:, columns], weights[:, columns], MULT)
+            nc.vector.tensor_reduce(mixed[:, stories], by_story(values[:, columns]), axis=X, op=ADD)
+
+        inverse = held.tile([P, STORIES], F32, name="inverse")
+        nc.vector.reciprocal(inverse[:], total[:])
         answer = held.tile([P, STORIES], F32, name="answer")
-        nc.vector.tensor_tensor(answer[:], mixed[:], state[:], ADD)
+        nc.vector.tensor_tensor(answer[:], mixed[:], inverse[:], MULT)
+        nc.vector.tensor_tensor(answer[:], answer[:], state[:], ADD)
         nc.sync.dma_start(out, answer[:])

@@ -50,12 +50,14 @@ def tile_memnnlayer_kernel(tc, table, ta, tc_enc, u, offs, out):
         nc.scalar.activation(warm[:], warm[:], EXP)
         key_time_all = held.tile([P, SENTENCES], F32, name="key_time_all")
         nc.vector.tensor_copy(by_story(key_time_all[:]), key_time[:].unsqueeze(1).to_broadcast([P, STORIES, SLOTS]))
-        value_shift = held.tile([P, GROUP_COLUMNS], F32, name="value_shift")
+        time_shift = held.tile([P, SLOTS], F32, name="time_shift")
+        nc.gpsimd.tensor_tensor(time_shift[:], value_time[:], key_time[:], SUBTRACT)
+        value_shift = held.tile([P, SENTENCES], F32, name="value_shift")
         nc.gpsimd.tensor_tensor(
             by_story(value_shift[:]),
-            value_time[:].unsqueeze(1).to_broadcast([P, GROUP, SLOTS]),
-            key_time[:].unsqueeze(1).to_broadcast([P, GROUP, SLOTS]),
-            SUBTRACT,
+            time_shift[:].unsqueeze(1).to_broadcast([P, STORIES, SLOTS]),
+            state[:].unsqueeze(2).to_broadcast([P, STORIES, SLOTS]),
+            ADD,
         )
         state_wide = held.tile([P, STORIES * P], BF16, name="state_wide")
         nc.scalar.activation(
@@ -76,40 +78,52 @@ def tile_memnnlayer_kernel(tc, table, ta, tc_enc, u, offs, out):
         keys_bf = held.tile([P, SENTENCES], BF16, name="keys_bf")
         values = held.tile([P, SENTENCES], F32, name="values")
         weights = held.tile([P, SENTENCES], F32, name="weights")
+        products = held.tile([P, SENTENCES], F32, name="products")
         neg_max = held.tile([P, STORIES], F32, name="neg_max")
         total = held.tile([P, STORIES], F32, name="total")
         mixed = held.tile([P, STORIES], F32, name="mixed")
+        scores = [psum.tile([P, GROUP_COLUMNS], F32, name=f"score{g}") for g in range(GROUPS)]
         for g in range(GROUPS):
             columns = slice(g * GROUP_COLUMNS, (g + 1) * GROUP_COLUMNS)
-            stories = slice(g * GROUP, (g + 1) * GROUP)
-            nc.scalar.copy(keys_bf[:, columns], keys[:, columns])
-            nc.gpsimd.tensor_tensor(values[:, columns], keys[:, columns], value_shift[:], ADD)
-            score = psum.tile([P, GROUP_COLUMNS], F32, name=f"score{g}")
+            if g < GROUPS - 1:
+                nc.scalar.copy(keys_bf[:, columns], keys[:, columns])
+            else:
+                nc.vector.tensor_copy(keys_bf[:, columns], keys[:, columns])
+            nc.gpsimd.tensor_tensor(values[:, columns], keys[:, columns], value_shift[:, columns], ADD)
             for j in range(GROUP):
                 b = g * GROUP + j
                 nc.tensor.matmul(
-                    score[:, j * SLOTS : (j + 1) * SLOTS],
+                    scores[g][:, j * SLOTS : (j + 1) * SLOTS],
                     state_wide[:, b * P : (b + 1) * P],
                     keys_bf[:, b * SLOTS : (b + 1) * SLOTS],
                     start=True,
                     stop=True,
                 )
-            nc.vector.tensor_reduce(neg_max[:, stories], by_story(score[:]), axis=X, op=MAX, negate=True)
+        for g in range(GROUPS):
+            stories = slice(g * GROUP, (g + 1) * GROUP)
+            nc.vector.tensor_reduce(neg_max[:, stories], by_story(scores[g][:]), axis=X, op=MAX, negate=True)
             for j in range(GROUP):
                 b = g * GROUP + j
+                slots = slice(b * SLOTS, (b + 1) * SLOTS)
                 nc.scalar.activation(
-                    weights[:, b * SLOTS : (b + 1) * SLOTS],
-                    score[:, j * SLOTS : (j + 1) * SLOTS],
+                    weights[:, slots],
+                    scores[g][:, j * SLOTS : (j + 1) * SLOTS],
                     EXP,
                     bias=neg_max[:, b : b + 1],
                     accum_out=total[:, b : b + 1],
                 )
-            nc.vector.tensor_tensor(values[:, columns], values[:, columns], weights[:, columns], MULT)
-            nc.vector.tensor_reduce(mixed[:, stories], by_story(values[:, columns]), axis=X, op=ADD)
+                nc.vector.scalar_tensor_tensor(
+                    out=products[:, slots],
+                    in0=weights[:, slots],
+                    scalar=1.0,
+                    in1=values[:, slots],
+                    op0=MULT,
+                    op1=MULT,
+                    accum_out=mixed[:, b : b + 1],
+                )
 
         inverse = held.tile([P, STORIES], F32, name="inverse")
         nc.vector.reciprocal(inverse[:], total[:])
         answer = held.tile([P, STORIES], F32, name="answer")
         nc.vector.tensor_tensor(answer[:], mixed[:], inverse[:], MULT)
-        nc.vector.tensor_tensor(answer[:], answer[:], state[:], ADD)
         nc.sync.dma_start(out, answer[:])

@@ -78,52 +78,39 @@ def tile_memnnlayer_kernel(tc, table, ta, tc_enc, u, offs, out):
         keys_bf = held.tile([P, SENTENCES], BF16, name="keys_bf")
         values = held.tile([P, SENTENCES], F32, name="values")
         weights = held.tile([P, SENTENCES], F32, name="weights")
-        products = held.tile([P, SENTENCES], F32, name="products")
         neg_max = held.tile([P, STORIES], F32, name="neg_max")
         total = held.tile([P, STORIES], F32, name="total")
         mixed = held.tile([P, STORIES], F32, name="mixed")
-        scores = [psum.tile([P, GROUP_COLUMNS], F32, name=f"score{g}") for g in range(GROUPS)]
+        inverse = held.tile([P, STORIES], F32, name="inverse")
         for g in range(GROUPS):
             columns = slice(g * GROUP_COLUMNS, (g + 1) * GROUP_COLUMNS)
-            if g < GROUPS - 1:
-                nc.scalar.copy(keys_bf[:, columns], keys[:, columns])
-            else:
-                nc.vector.tensor_copy(keys_bf[:, columns], keys[:, columns])
+            stories = slice(g * GROUP, (g + 1) * GROUP)
+            nc.scalar.copy(keys_bf[:, columns], keys[:, columns])
             nc.gpsimd.tensor_tensor(values[:, columns], keys[:, columns], value_shift[:, columns], ADD)
+            score = psum.tile([P, GROUP_COLUMNS], F32, name=f"score{g}")
             for j in range(GROUP):
                 b = g * GROUP + j
                 nc.tensor.matmul(
-                    scores[g][:, j * SLOTS : (j + 1) * SLOTS],
+                    score[:, j * SLOTS : (j + 1) * SLOTS],
                     state_wide[:, b * P : (b + 1) * P],
                     keys_bf[:, b * SLOTS : (b + 1) * SLOTS],
                     start=True,
                     stop=True,
                 )
-        for g in range(GROUPS):
-            stories = slice(g * GROUP, (g + 1) * GROUP)
-            nc.vector.tensor_reduce(neg_max[:, stories], by_story(scores[g][:]), axis=X, op=MAX, negate=True)
+            nc.vector.tensor_reduce(neg_max[:, stories], by_story(score[:]), axis=X, op=MAX, negate=True)
             for j in range(GROUP):
                 b = g * GROUP + j
-                slots = slice(b * SLOTS, (b + 1) * SLOTS)
                 nc.scalar.activation(
-                    weights[:, slots],
-                    scores[g][:, j * SLOTS : (j + 1) * SLOTS],
+                    weights[:, b * SLOTS : (b + 1) * SLOTS],
+                    score[:, j * SLOTS : (j + 1) * SLOTS],
                     EXP,
                     bias=neg_max[:, b : b + 1],
-                    accum_out=total[:, b : b + 1],
                 )
-                nc.vector.scalar_tensor_tensor(
-                    out=products[:, slots],
-                    in0=weights[:, slots],
-                    scalar=1.0,
-                    in1=values[:, slots],
-                    op0=MULT,
-                    op1=MULT,
-                    accum_out=mixed[:, b : b + 1],
-                )
+            nc.vector.tensor_reduce(total[:, stories], by_story(weights[:, columns]), axis=X, op=ADD)
+            nc.vector.tensor_tensor(values[:, columns], values[:, columns], weights[:, columns], MULT)
+            nc.vector.reciprocal(inverse[:, stories], total[:, stories])
+            nc.vector.tensor_reduce(mixed[:, stories], by_story(values[:, columns]), axis=X, op=ADD)
 
-        inverse = held.tile([P, STORIES], F32, name="inverse")
-        nc.vector.reciprocal(inverse[:], total[:])
         answer = held.tile([P, STORIES], F32, name="answer")
         nc.vector.tensor_tensor(answer[:], mixed[:], inverse[:], MULT)
         nc.sync.dma_start(out, answer[:])

@@ -17,7 +17,7 @@ STORIES = 16
 SLOTS = 32
 WORDS = 4
 SENTENCES = STORIES * SLOTS
-GROUP = 4
+GROUP = 8
 GROUPS = STORIES // GROUP
 GROUP_COLUMNS = GROUP * SLOTS
 LOAD_PIECES = 4
@@ -67,11 +67,10 @@ def tile_memnnlayer_kernel(tc, table, ta, tc_enc, u, offs, out):
         sums = [held.tile([P, SENTENCES], F32, name=f"sums{i}") for i in range(2)]
         keys = key_time_all
         for t in range(WORDS):
-            width = GROUP_COLUMNS if t == WORDS - 1 else SENTENCES
-            for start in range(0, SENTENCES, width):
-                columns = slice(start, start + width)
-                first = (t * SENTENCES + start) // 16
-                picked = words[:].indirect(offsets[:, first : first + width // 16])
+            for g in range(GROUPS):
+                columns = slice(g * GROUP_COLUMNS, (g + 1) * GROUP_COLUMNS)
+                first = (t * SENTENCES + g * GROUP_COLUMNS) // 16
+                picked = words[:].indirect(offsets[:, first : first + GROUP_COLUMNS // 16])
                 nc.vector.tensor_tensor(sums[t % 2][:, columns], picked, keys[:, columns], ADD)
             keys = sums[t % 2]
 
@@ -105,12 +104,12 @@ def tile_memnnlayer_kernel(tc, table, ta, tc_enc, u, offs, out):
                     score[:, j * SLOTS : (j + 1) * SLOTS],
                     EXP,
                     bias=neg_max[:, b : b + 1],
+                    accum_out=total[:, b : b + 1],
                 )
-            nc.vector.tensor_reduce(total[:, stories], by_story(weights[:, columns]), axis=X, op=ADD)
             nc.vector.tensor_tensor(values[:, columns], values[:, columns], weights[:, columns], MULT)
-            nc.vector.reciprocal(inverse[:, stories], total[:, stories])
             nc.vector.tensor_reduce(mixed[:, stories], by_story(values[:, columns]), axis=X, op=ADD)
 
+        nc.vector.reciprocal(inverse[:], total[:])
         answer = held.tile([P, STORIES], F32, name="answer")
         nc.vector.tensor_tensor(answer[:], mixed[:], inverse[:], MULT)
         nc.sync.dma_start(out, answer[:])

@@ -74,7 +74,7 @@ def tile_memnnlayer_kernel(tc, table, ta, tc_enc, u, offs, out):
                 nc.vector.tensor_tensor(sums[t % 2][:, columns], picked, keys[:, columns], ADD)
             keys = sums[t % 2]
 
-        keys_bf = held.tile([P, SENTENCES], BF16, name="keys_bf")
+        keys_bf = keys[:].bitcast(BF16).rearrange("e (c half) -> e c half", half=2)[:, :, 1]
         values = held.tile([P, SENTENCES], F32, name="values")
         weights = held.tile([P, SENTENCES], F32, name="weights")
         neg_max = held.tile([P, STORIES], F32, name="neg_max")
@@ -84,7 +84,6 @@ def tile_memnnlayer_kernel(tc, table, ta, tc_enc, u, offs, out):
         for g in range(GROUPS):
             columns = slice(g * GROUP_COLUMNS, (g + 1) * GROUP_COLUMNS)
             stories = slice(g * GROUP, (g + 1) * GROUP)
-            nc.scalar.copy(keys_bf[:, columns], keys[:, columns])
             nc.gpsimd.tensor_tensor(values[:, columns], keys[:, columns], value_shift[:, columns], ADD)
             score = psum.tile([P, GROUP_COLUMNS], F32, name=f"score{g}")
             for j in range(GROUP):

@@ -84,7 +84,7 @@ def tile_memnnlayer_kernel(tc, table, ta, tc_enc, u, offs, out):
         for g in range(GROUPS):
             columns = slice(g * GROUP_COLUMNS, (g + 1) * GROUP_COLUMNS)
             stories = slice(g * GROUP, (g + 1) * GROUP)
-            nc.gpsimd.tensor_tensor(values[:, columns], keys[:, columns], value_shift[:, columns], ADD)
+            nc.vector.tensor_tensor(values[:, columns], keys[:, columns], value_shift[:, columns], ADD)
             score = psum.tile([P, GROUP_COLUMNS], F32, name=f"score{g}")
             for j in range(GROUP):
                 b = g * GROUP + j

@@ -21,6 +21,7 @@ GROUP = 8
 GROUPS = STORIES // GROUP
 GROUP_COLUMNS = GROUP * SLOTS
 LOAD_PIECES = 4
+BANK = 512
 
 FLOPS = 2 * P * SENTENCES * 2
 
@@ -30,17 +31,17 @@ def tile_memnnlayer_kernel(tc, table, ta, tc_enc, u, offs, out):
     with tc.tile_pool(name="held", bufs=1) as held, tc.psum_pool(name="psum", bufs=1) as psum:
         offsets = held.tile([P, WORDS * SENTENCES // 16], U16, name="offsets")
         nc.sync.dma_start(offsets[:], offs)
-        key_time = held.tile([P, SLOTS], F32, name="key_time")
-        nc.scalar.dma_start(key_time[:], ta)
+        value_time = held.tile([P, SLOTS], F32, name="value_time")
+        nc.scalar.dma_start(value_time[:], tc_enc)
+        state = held.tile([P, STORIES], F32, name="state")
+        nc.sync.dma_start(state[:], u)
         words = held.tile([P, VOCAB], F32, name="words")
         piece = VOCAB // LOAD_PIECES
         for i in range(LOAD_PIECES):
-            queue = nc.sync if i % 2 == 0 else nc.scalar
+            queue = nc.scalar if i % 2 == 0 else nc.sync
             queue.dma_start(words[:, i * piece : (i + 1) * piece], table[:, i * piece : (i + 1) * piece])
-        state = held.tile([P, STORIES], F32, name="state")
-        nc.sync.dma_start(state[:], u)
-        value_time = held.tile([P, SLOTS], F32, name="value_time")
-        nc.scalar.dma_start(value_time[:], tc_enc)
+        key_time = held.tile([P, SLOTS], F32, name="key_time")
+        nc.scalar.dma_start(key_time[:], ta)
 
         def by_story(ap):
             return ap.rearrange("e (b s) -> e b s", s=SLOTS)
@@ -48,34 +49,42 @@ def tile_memnnlayer_kernel(tc, table, ta, tc_enc, u, offs, out):
         warm = held.tile([P, 1], F32, name="warm")
         nc.vector.memset(warm[:], 0.0)
         nc.scalar.activation(warm[:], warm[:], EXP)
-        key_time_all = held.tile([P, SENTENCES], F32, name="key_time_all")
-        nc.vector.tensor_copy(by_story(key_time_all[:]), key_time[:].unsqueeze(1).to_broadcast([P, STORIES, SLOTS]))
-        time_shift = held.tile([P, SLOTS], F32, name="time_shift")
-        nc.gpsimd.tensor_tensor(time_shift[:], value_time[:], key_time[:], SUBTRACT)
-        value_shift = held.tile([P, SENTENCES], F32, name="value_shift")
-        nc.gpsimd.tensor_tensor(
-            by_story(value_shift[:]),
-            time_shift[:].unsqueeze(1).to_broadcast([P, STORIES, SLOTS]),
+        values_start = held.tile([P, SENTENCES], F32, name="values_start")
+        nc.vector.tensor_tensor(
+            by_story(values_start[:]),
+            value_time[:].unsqueeze(1).to_broadcast([P, STORIES, SLOTS]),
             state[:].unsqueeze(2).to_broadcast([P, STORIES, SLOTS]),
             ADD,
         )
+        time_shift = held.tile([P, SLOTS], BF16, name="time_shift")
+        nc.gpsimd.tensor_tensor(time_shift[:], key_time[:], value_time[:], SUBTRACT)
         state_wide = held.tile([P, STORIES * P], BF16, name="state_wide")
         nc.scalar.activation(
             state_wide[:].rearrange("e (b r) -> e b r", r=P), state[:].unsqueeze(2).to_broadcast([P, STORIES, P]), COPY
         )
+        scores = [psum.tile([P, BANK], F32, name=f"scores{g}") for g in range(GROUPS)]
+        for g in range(GROUPS):
+            for j in range(GROUP):
+                b = g * GROUP + j
+                nc.tensor.matmul(
+                    scores[g][:, j * SLOTS : (j + 1) * SLOTS],
+                    state_wide[:, b * P : (b + 1) * P],
+                    time_shift[:],
+                    start=(j == 0),
+                    stop=False,
+                )
 
         sums = [held.tile([P, SENTENCES], F32, name=f"sums{i}") for i in range(2)]
-        keys = key_time_all
+        values = values_start
         for t in range(WORDS):
             for g in range(GROUPS):
                 columns = slice(g * GROUP_COLUMNS, (g + 1) * GROUP_COLUMNS)
                 first = (t * SENTENCES + g * GROUP_COLUMNS) // 16
                 picked = words[:].indirect(offsets[:, first : first + GROUP_COLUMNS // 16])
-                nc.vector.tensor_tensor(sums[t % 2][:, columns], picked, keys[:, columns], ADD)
-            keys = sums[t % 2]
+                nc.vector.tensor_tensor(sums[t % 2][:, columns], picked, values[:, columns], ADD)
+            values = sums[t % 2]
 
-        keys_bf = keys[:].bitcast(BF16).rearrange("e (c half) -> e c half", half=2)[:, :, 1]
-        values = held.tile([P, SENTENCES], F32, name="values")
+        values_bf = values[:].bitcast(BF16).rearrange("e (c half) -> e c half", half=2)[:, :, 1]
         weights = held.tile([P, SENTENCES], F32, name="weights")
         neg_max = held.tile([P, STORIES], F32, name="neg_max")
         total = held.tile([P, STORIES], F32, name="total")
@@ -84,29 +93,29 @@ def tile_memnnlayer_kernel(tc, table, ta, tc_enc, u, offs, out):
         for g in range(GROUPS):
             columns = slice(g * GROUP_COLUMNS, (g + 1) * GROUP_COLUMNS)
             stories = slice(g * GROUP, (g + 1) * GROUP)
-            nc.vector.tensor_tensor(values[:, columns], keys[:, columns], value_shift[:, columns], ADD)
-            score = psum.tile([P, GROUP_COLUMNS], F32, name=f"score{g}")
             for j in range(GROUP):
                 b = g * GROUP + j
                 nc.tensor.matmul(
-                    score[:, j * SLOTS : (j + 1) * SLOTS],
+                    scores[g][:, j * SLOTS : (j + 1) * SLOTS],
                     state_wide[:, b * P : (b + 1) * P],
-                    keys_bf[:, b * SLOTS : (b + 1) * SLOTS],
-                    start=True,
-                    stop=True,
+                    values_bf[:, b * SLOTS : (b + 1) * SLOTS],
+                    start=False,
+                    stop=(j == GROUP - 1),
                 )
-            nc.vector.tensor_reduce(neg_max[:, stories], by_story(score[:]), axis=X, op=MAX, negate=True)
+            nc.vector.tensor_reduce(
+                neg_max[:, stories], by_story(scores[g][:, :GROUP_COLUMNS]), axis=X, op=MAX, negate=True
+            )
             for j in range(GROUP):
                 b = g * GROUP + j
                 nc.scalar.activation(
                     weights[:, b * SLOTS : (b + 1) * SLOTS],
-                    score[:, j * SLOTS : (j + 1) * SLOTS],
+                    scores[g][:, j * SLOTS : (j + 1) * SLOTS],
                     EXP,
                     bias=neg_max[:, b : b + 1],
                     accum_out=total[:, b : b + 1],
                 )
-            nc.vector.tensor_tensor(values[:, columns], values[:, columns], weights[:, columns], MULT)
-            nc.vector.tensor_reduce(mixed[:, stories], by_story(values[:, columns]), axis=X, op=ADD)
+            nc.vector.tensor_tensor(weights[:, columns], weights[:, columns], values[:, columns], MULT)
+            nc.vector.tensor_reduce(mixed[:, stories], by_story(weights[:, columns]), axis=X, op=ADD)
 
         nc.vector.reciprocal(inverse[:], total[:])
         answer = held.tile([P, STORIES], F32, name="answer")

@@ -57,7 +57,7 @@ def tile_memnnlayer_kernel(tc, table, ta, tc_enc, u, offs, out):
             ADD,
         )
         time_shift = held.tile([P, SLOTS], BF16, name="time_shift")
-        nc.gpsimd.tensor_tensor(time_shift[:], key_time[:], value_time[:], SUBTRACT)
+        nc.vector.tensor_tensor(time_shift[:], key_time[:], value_time[:], SUBTRACT)
         state_wide = held.tile([P, STORIES * P], BF16, name="state_wide")
         nc.scalar.activation(
             state_wide[:].rearrange("e (b r) -> e b r", r=P), state[:].unsqueeze(2).to_broadcast([P, STORIES, P]), COPY

@@ -17,9 +17,9 @@ STORIES = 16
 SLOTS = 32
 WORDS = 4
 SENTENCES = STORIES * SLOTS
-GROUP = 8
-GROUPS = STORIES // GROUP
-GROUP_COLUMNS = GROUP * SLOTS
+SHARES = (4, 4, 4, 4)
+FIRST_STORY = (0, 4, 8, 12)
+LANES = 2
 LOAD_PIECES = 4
 BANK = 512
 
@@ -28,20 +28,24 @@ FLOPS = 2 * P * SENTENCES * 2
 
 def tile_memnnlayer_kernel(tc, table, ta, tc_enc, u, offs, out):
     nc = tc.nc
-    with tc.tile_pool(name="held", bufs=1) as held, tc.psum_pool(name="psum", bufs=1) as psum:
+    with (
+        tc.tile_pool(name="held", bufs=1) as held,
+        tc.tile_pool(name="ring", bufs=2) as ring,
+        tc.psum_pool(name="psum", bufs=1) as psum,
+    ):
         offsets = held.tile([P, WORDS * SENTENCES // 16], U16, name="offsets")
         nc.sync.dma_start(offsets[:], offs)
         value_time = held.tile([P, SLOTS], F32, name="value_time")
         nc.scalar.dma_start(value_time[:], tc_enc)
         state = held.tile([P, STORIES], F32, name="state")
         nc.sync.dma_start(state[:], u)
+        key_time = held.tile([P, SLOTS], F32, name="key_time")
+        nc.scalar.dma_start(key_time[:], ta)
         words = held.tile([P, VOCAB], F32, name="words")
         piece = VOCAB // LOAD_PIECES
         for i in range(LOAD_PIECES):
             queue = nc.scalar if i % 2 == 0 else nc.sync
             queue.dma_start(words[:, i * piece : (i + 1) * piece], table[:, i * piece : (i + 1) * piece])
-        key_time = held.tile([P, SLOTS], F32, name="key_time")
-        nc.scalar.dma_start(key_time[:], ta)
 
         def by_story(ap):
             return ap.rearrange("e (b s) -> e b s", s=SLOTS)
@@ -59,63 +63,88 @@ def tile_memnnlayer_kernel(tc, table, ta, tc_enc, u, offs, out):
         time_shift = held.tile([P, SLOTS], BF16, name="time_shift")
         nc.vector.tensor_tensor(time_shift[:], key_time[:], value_time[:], SUBTRACT)
         state_wide = held.tile([P, STORIES * P], BF16, name="state_wide")
-        nc.scalar.activation(
-            state_wide[:].rearrange("e (b r) -> e b r", r=P), state[:].unsqueeze(2).to_broadcast([P, STORIES, P]), COPY
-        )
-        scores = [psum.tile([P, BANK], F32, name=f"scores{g}") for g in range(GROUPS)]
-        for g in range(GROUPS):
-            for j in range(GROUP):
-                b = g * GROUP + j
+        for i, share in enumerate(SHARES):
+            stories = slice(FIRST_STORY[i], FIRST_STORY[i] + share)
+            nc.scalar.activation(
+                state_wide[:, stories.start * P : stories.stop * P].rearrange("e (b r) -> e b r", r=P),
+                state[:, stories].unsqueeze(2).to_broadcast([P, share, P]),
+                COPY,
+            )
+        scores = [psum.tile([P, BANK], F32, name=f"scores{i}") for i in range(len(SHARES))]
+        for i, share in enumerate(SHARES):
+            for j in range(share):
+                b = FIRST_STORY[i] + j
                 nc.tensor.matmul(
-                    scores[g][:, j * SLOTS : (j + 1) * SLOTS],
+                    scores[i][:, j * SLOTS : (j + 1) * SLOTS],
                     state_wide[:, b * P : (b + 1) * P],
                     time_shift[:],
                     start=(j == 0),
                     stop=False,
                 )
 
-        sums = [held.tile([P, SENTENCES], F32, name=f"sums{i}") for i in range(2)]
-        values = values_start
-        for t in range(WORDS):
-            for g in range(GROUPS):
-                columns = slice(g * GROUP_COLUMNS, (g + 1) * GROUP_COLUMNS)
-                first = (t * SENTENCES + g * GROUP_COLUMNS) // 16
-                picked = words[:].indirect(offsets[:, first : first + GROUP_COLUMNS // 16])
-                nc.vector.tensor_tensor(sums[t % 2][:, columns], picked, values[:, columns], ADD)
-            values = sums[t % 2]
-
+        values = held.tile([P, SENTENCES], F32, name="values")
         values_bf = values[:].bitcast(BF16).rearrange("e (c half) -> e c half", half=2)[:, :, 1]
         weights = held.tile([P, SENTENCES], F32, name="weights")
         neg_max = held.tile([P, STORIES], F32, name="neg_max")
         total = held.tile([P, STORIES], F32, name="total")
         mixed = held.tile([P, STORIES], F32, name="mixed")
         inverse = held.tile([P, STORIES], F32, name="inverse")
-        for g in range(GROUPS):
-            columns = slice(g * GROUP_COLUMNS, (g + 1) * GROUP_COLUMNS)
-            stories = slice(g * GROUP, (g + 1) * GROUP)
-            for j in range(GROUP):
-                b = g * GROUP + j
+
+        def columns_of(i):
+            return slice(FIRST_STORY[i] * SLOTS, (FIRST_STORY[i] + SHARES[i]) * SLOTS)
+
+        def stories_of(i):
+            return slice(FIRST_STORY[i], FIRST_STORY[i] + SHARES[i])
+
+        def look_up(i, t, before):
+            columns = columns_of(i)
+            first = (t * SENTENCES + columns.start) // 16
+            picked = words[:].indirect(offsets[:, first : first + SHARES[i] * SLOTS // 16])
+            if t == WORDS - 1:
+                after = values[:, columns]
+            else:
+                partial = ring.tile([P, SHARES[i] * SLOTS], F32, name=f"lane{i % LANES}")
+                after = partial[:]
+            nc.vector.tensor_tensor(after, picked, before, ADD)
+            return after
+
+        def soften(i):
+            for j in range(SHARES[i]):
+                b = FIRST_STORY[i] + j
                 nc.tensor.matmul(
-                    scores[g][:, j * SLOTS : (j + 1) * SLOTS],
+                    scores[i][:, j * SLOTS : (j + 1) * SLOTS],
                     state_wide[:, b * P : (b + 1) * P],
                     values_bf[:, b * SLOTS : (b + 1) * SLOTS],
                     start=False,
-                    stop=(j == GROUP - 1),
+                    stop=(j == SHARES[i] - 1),
                 )
             nc.vector.tensor_reduce(
-                neg_max[:, stories], by_story(scores[g][:, :GROUP_COLUMNS]), axis=X, op=MAX, negate=True
+                neg_max[:, stories_of(i)], by_story(scores[i][:, : SHARES[i] * SLOTS]), axis=X, op=MAX, negate=True
             )
-            for j in range(GROUP):
-                b = g * GROUP + j
+            for j in range(SHARES[i]):
+                b = FIRST_STORY[i] + j
                 nc.scalar.activation(
                     weights[:, b * SLOTS : (b + 1) * SLOTS],
-                    scores[g][:, j * SLOTS : (j + 1) * SLOTS],
+                    scores[i][:, j * SLOTS : (j + 1) * SLOTS],
                     EXP,
                     bias=neg_max[:, b : b + 1],
                     accum_out=total[:, b : b + 1],
                 )
+
+        def mix(i):
+            columns = columns_of(i)
             nc.vector.tensor_tensor(weights[:, columns], weights[:, columns], values[:, columns], MULT)
-            nc.vector.tensor_reduce(mixed[:, stories], by_story(weights[:, columns]), axis=X, op=ADD)
+            nc.vector.tensor_reduce(mixed[:, stories_of(i)], by_story(weights[:, columns]), axis=X, op=ADD)
+
+        for first_share in range(0, len(SHARES), LANES):
+            together = range(first_share, first_share + LANES)
+            sums = [values_start[:, columns_of(i)] for i in together]
+            for t in range(WORDS):
+                sums = [look_up(i, t, before) for i, before in zip(together, sums)]
+            for i in together:
+                soften(i)
+        for i in range(len(SHARES)):
+            mix(i)
 
         nc.vector.reciprocal(inverse[:], total[:])
         answer = held.tile([P, STORIES], F32, name="answer")

@@ -17,9 +17,11 @@ STORIES = 16
 SLOTS = 32
 WORDS = 4
 SENTENCES = STORIES * SLOTS
-SHARES = (4, 4, 4, 4)
-FIRST_STORY = (0, 4, 8, 12)
+PIECE = 4
 LANES = 2
+BATCH = LANES * PIECE
+SHARES = (4, 4, 4, 2, 2)
+FIRST_STORY = (0, 4, 8, 12, 14)
 LOAD_PIECES = 4
 BANK = 512
 
@@ -96,14 +98,13 @@ def tile_memnnlayer_kernel(tc, table, ta, tc_enc, u, offs, out):
         def stories_of(i):
             return slice(FIRST_STORY[i], FIRST_STORY[i] + SHARES[i])
 
-        def look_up(i, t, before):
-            columns = columns_of(i)
-            first = (t * SENTENCES + columns.start) // 16
-            picked = words[:].indirect(offsets[:, first : first + SHARES[i] * SLOTS // 16])
+        def look_up(k, t, before):
+            first = (t * SENTENCES + k * PIECE * SLOTS) // 16
+            picked = words[:].indirect(offsets[:, first : first + PIECE * SLOTS // 16])
             if t == WORDS - 1:
-                after = values[:, columns]
+                after = values[:, k * PIECE * SLOTS : (k + 1) * PIECE * SLOTS]
             else:
-                partial = ring.tile([P, SHARES[i] * SLOTS], F32, name=f"lane{i % LANES}")
+                partial = ring.tile([P, PIECE * SLOTS], F32, name=f"lane{k % LANES}")
                 after = partial[:]
             nc.vector.tensor_tensor(after, picked, before, ADD)
             return after
@@ -136,13 +137,14 @@ def tile_memnnlayer_kernel(tc, table, ta, tc_enc, u, offs, out):
             nc.vector.tensor_tensor(weights[:, columns], weights[:, columns], values[:, columns], MULT)
             nc.vector.tensor_reduce(mixed[:, stories_of(i)], by_story(weights[:, columns]), axis=X, op=ADD)
 
-        for first_share in range(0, len(SHARES), LANES):
-            together = range(first_share, first_share + LANES)
-            sums = [values_start[:, columns_of(i)] for i in together]
+        for batch in range(STORIES // BATCH):
+            together = range(batch * LANES, (batch + 1) * LANES)
+            sums = [values_start[:, k * PIECE * SLOTS : (k + 1) * PIECE * SLOTS] for k in together]
             for t in range(WORDS):
-                sums = [look_up(i, t, before) for i, before in zip(together, sums)]
-            for i in together:
-                soften(i)
+                sums = [look_up(k, t, before) for k, before in zip(together, sums)]
+            for i in range(len(SHARES)):
+                if FIRST_STORY[i] // BATCH == batch:
+                    soften(i)
         for i in range(len(SHARES)):
             mix(i)
 

@@ -17,7 +17,7 @@ STORIES = 16
 SLOTS = 32
 WORDS = 4
 SENTENCES = STORIES * SLOTS
-PIECE = 4
+PIECE = 8
 LANES = 2
 BATCH = LANES * PIECE
 SHARES = (4, 4, 4, 2, 2)

@@ -35,19 +35,18 @@ def tile_memnnlayer_kernel(tc, table, ta, tc_enc, u, offs, out):
         tc.tile_pool(name="ring", bufs=2) as ring,
         tc.psum_pool(name="psum", bufs=1) as psum,
     ):
+        words = held.tile([P, VOCAB], F32, name="words")
+        part = VOCAB // LOAD_PIECES
+        for i in range(LOAD_PIECES):
+            nc.sync.dma_start(words[:, i * part : (i + 1) * part], table[:, i * part : (i + 1) * part])
         offsets = held.tile([P, WORDS * SENTENCES // 16], U16, name="offsets")
         nc.sync.dma_start(offsets[:], offs)
+        state = held.tile([P, STORIES], F32, name="state")
+        nc.scalar.dma_start(state[:], u)
         value_time = held.tile([P, SLOTS], F32, name="value_time")
         nc.scalar.dma_start(value_time[:], tc_enc)
-        state = held.tile([P, STORIES], F32, name="state")
-        nc.sync.dma_start(state[:], u)
         key_time = held.tile([P, SLOTS], F32, name="key_time")
         nc.scalar.dma_start(key_time[:], ta)
-        words = held.tile([P, VOCAB], F32, name="words")
-        piece = VOCAB // LOAD_PIECES
-        for i in range(LOAD_PIECES):
-            queue = nc.scalar if i % 2 == 0 else nc.sync
-            queue.dma_start(words[:, i * piece : (i + 1) * piece], table[:, i * piece : (i + 1) * piece])
 
         def by_story(ap):
             return ap.rearrange("e (b s) -> e b s", s=SLOTS)

@@ -55,12 +55,14 @@ def tile_memnnlayer_kernel(tc, table, ta, tc_enc, u, offs, out):
         nc.vector.memset(warm[:], 0.0)
         nc.scalar.activation(warm[:], warm[:], EXP)
         values_start = held.tile([P, SENTENCES], F32, name="values_start")
-        nc.vector.tensor_tensor(
-            by_story(values_start[:]),
-            value_time[:].unsqueeze(1).to_broadcast([P, STORIES, SLOTS]),
-            state[:].unsqueeze(2).to_broadcast([P, STORIES, SLOTS]),
-            ADD,
-        )
+        for k in range(LANES):
+            stories = slice(k * PIECE, (k + 1) * PIECE)
+            nc.vector.tensor_tensor(
+                by_story(values_start[:, k * PIECE * SLOTS : (k + 1) * PIECE * SLOTS]),
+                value_time[:].unsqueeze(1).to_broadcast([P, PIECE, SLOTS]),
+                state[:, stories].unsqueeze(2).to_broadcast([P, PIECE, SLOTS]),
+                ADD,
+            )
         time_shift = held.tile([P, SLOTS], BF16, name="time_shift")
         nc.vector.tensor_tensor(time_shift[:], key_time[:], value_time[:], SUBTRACT)
         state_wide = held.tile([P, STORIES * P], BF16, name="state_wide")

import concourse.mybir as mybir

F32 = mybir.dt.float32
BF16 = mybir.dt.bfloat16
U16 = mybir.dt.uint16
ADD = mybir.AluOpType.add
SUBTRACT = mybir.AluOpType.subtract
MULT = mybir.AluOpType.mult
MAX = mybir.AluOpType.max
EXP = mybir.ActivationFunctionType.Exp
COPY = mybir.ActivationFunctionType.Copy
X = mybir.AxisListType.X

P = 128
VOCAB = 1024
STORIES = 16
SLOTS = 32
WORDS = 4
SENTENCES = STORIES * SLOTS
PIECE = 8
LANES = 2
BATCH = LANES * PIECE
SHARES = (4, 4, 4, 2, 2)
FIRST_STORY = (0, 4, 8, 12, 14)
LOAD_PIECES = 4
BANK = 512

FLOPS = 2 * P * SENTENCES * 2


def tile_memnnlayer_kernel(tc, table, ta, tc_enc, u, offs, out):
    nc = tc.nc
    with (
        tc.tile_pool(name="held", bufs=1) as held,
        tc.tile_pool(name="ring", bufs=2) as ring,
        tc.psum_pool(name="psum", bufs=1) as psum,
    ):
        words = held.tile([P, VOCAB], F32, name="words")
        part = VOCAB // LOAD_PIECES
        for i in range(LOAD_PIECES):
            nc.sync.dma_start(words[:, i * part : (i + 1) * part], table[:, i * part : (i + 1) * part])
        offsets = held.tile([P, WORDS * SENTENCES // 16], U16, name="offsets")
        nc.sync.dma_start(offsets[:], offs)
        state = held.tile([P, STORIES], F32, name="state")
        nc.scalar.dma_start(state[:], u)
        value_time = held.tile([P, SLOTS], F32, name="value_time")
        nc.scalar.dma_start(value_time[:], tc_enc)
        key_time = held.tile([P, SLOTS], F32, name="key_time")
        nc.scalar.dma_start(key_time[:], ta)

        def by_story(ap):
            return ap.rearrange("e (b s) -> e b s", s=SLOTS)

        warm = held.tile([P, 1], F32, name="warm")
        nc.vector.memset(warm[:], 0.0)
        nc.scalar.activation(warm[:], warm[:], EXP)
        values_start = held.tile([P, SENTENCES], F32, name="values_start")
        for k in range(LANES):
            stories = slice(k * PIECE, (k + 1) * PIECE)
            nc.vector.tensor_tensor(
                by_story(values_start[:, k * PIECE * SLOTS : (k + 1) * PIECE * SLOTS]),
                value_time[:].unsqueeze(1).to_broadcast([P, PIECE, SLOTS]),
                state[:, stories].unsqueeze(2).to_broadcast([P, PIECE, SLOTS]),
                ADD,
            )
        time_shift = held.tile([P, SLOTS], BF16, name="time_shift")
        nc.vector.tensor_tensor(time_shift[:], key_time[:], value_time[:], SUBTRACT)
        state_wide = held.tile([P, STORIES * P], BF16, name="state_wide")
        for i, share in enumerate(SHARES):
            stories = slice(FIRST_STORY[i], FIRST_STORY[i] + share)
            nc.scalar.activation(
                state_wide[:, stories.start * P : stories.stop * P].rearrange("e (b r) -> e b r", r=P),
                state[:, stories].unsqueeze(2).to_broadcast([P, share, P]),
                COPY,
            )
        scores = [psum.tile([P, BANK], F32, name=f"scores{i}") for i in range(len(SHARES))]
        for i, share in enumerate(SHARES):
            for j in range(share):
                b = FIRST_STORY[i] + j
                nc.tensor.matmul(
                    scores[i][:, j * SLOTS : (j + 1) * SLOTS],
                    state_wide[:, b * P : (b + 1) * P],
                    time_shift[:],
                    start=(j == 0),
                    stop=False,
                )

        values = held.tile([P, SENTENCES], F32, name="values")
        values_bf = values[:].bitcast(BF16).rearrange("e (c half) -> e c half", half=2)[:, :, 1]
        weights = held.tile([P, SENTENCES], F32, name="weights")
        neg_max = held.tile([P, STORIES], F32, name="neg_max")
        total = held.tile([P, STORIES], F32, name="total")
        mixed = held.tile([P, STORIES], F32, name="mixed")
        inverse = held.tile([P, STORIES], F32, name="inverse")

        def columns_of(i):
            return slice(FIRST_STORY[i] * SLOTS, (FIRST_STORY[i] + SHARES[i]) * SLOTS)

        def stories_of(i):
            return slice(FIRST_STORY[i], FIRST_STORY[i] + SHARES[i])

        def look_up(k, t, before):
            first = (t * SENTENCES + k * PIECE * SLOTS) // 16
            picked = words[:].indirect(offsets[:, first : first + PIECE * SLOTS // 16])
            if t == WORDS - 1:
                after = values[:, k * PIECE * SLOTS : (k + 1) * PIECE * SLOTS]
            else:
                partial = ring.tile([P, PIECE * SLOTS], F32, name=f"lane{k % LANES}")
                after = partial[:]
            nc.vector.tensor_tensor(after, picked, before, ADD)
            return after

        def soften(i):
            for j in range(SHARES[i]):
                b = FIRST_STORY[i] + j
                nc.tensor.matmul(
                    scores[i][:, j * SLOTS : (j + 1) * SLOTS],
                    state_wide[:, b * P : (b + 1) * P],
                    values_bf[:, b * SLOTS : (b + 1) * SLOTS],
                    start=False,
                    stop=(j == SHARES[i] - 1),
                )
            nc.vector.tensor_reduce(
                neg_max[:, stories_of(i)], by_story(scores[i][:, : SHARES[i] * SLOTS]), axis=X, op=MAX, negate=True
            )
            for j in range(SHARES[i]):
                b = FIRST_STORY[i] + j
                nc.scalar.activation(
                    weights[:, b * SLOTS : (b + 1) * SLOTS],
                    scores[i][:, j * SLOTS : (j + 1) * SLOTS],
                    EXP,
                    bias=neg_max[:, b : b + 1],
                    accum_out=total[:, b : b + 1],
                )

        def mix(i):
            columns = columns_of(i)
            nc.vector.tensor_tensor(weights[:, columns], weights[:, columns], values[:, columns], MULT)
            nc.vector.tensor_reduce(mixed[:, stories_of(i)], by_story(weights[:, columns]), axis=X, op=ADD)

        for batch in range(STORIES // BATCH):
            together = range(batch * LANES, (batch + 1) * LANES)
            sums = [values_start[:, k * PIECE * SLOTS : (k + 1) * PIECE * SLOTS] for k in together]
            for t in range(WORDS):
                sums = [look_up(k, t, before) for k, before in zip(together, sums)]
            for i in range(len(SHARES)):
                if FIRST_STORY[i] // BATCH == batch:
                    soften(i)
        for i in range(len(SHARES)):
            mix(i)

        nc.vector.reciprocal(inverse[:], total[:])
        answer = held.tile([P, STORIES], F32, name="answer")
        nc.vector.tensor_tensor(answer[:], mixed[:], inverse[:], MULT)
        nc.sync.dma_start(out, answer[:])
